import numpy as np
import ml_dtypes


def mxq(x, axis, fmt="e4m3"):
    dtype, down = {"e4m3": (ml_dtypes.float8_e4m3fn, 7), "e5m2": (ml_dtypes.float8_e5m2, 14)}[fmt]
    v = np.moveaxis(np.asarray(x, np.float32).astype(ml_dtypes.bfloat16).astype(np.float64), axis, -1)
    blocks = v.reshape(v.shape[:-1] + (-1, 32))
    amax = np.abs(blocks).max(-1, keepdims=True)
    byte = np.maximum(np.where(amax > 0, np.frexp(amax)[1] - 1 + 127, 0) - down, 1)
    scale = np.exp2(byte - 127.0)
    codes = (blocks / scale).astype(np.float32).astype(dtype).astype(np.float64)
    return np.moveaxis((codes * scale).reshape(v.shape), -1, axis)


WIDE = False


def mx_kscale(k):
    if not WIDE:
        return np.ones(k)
    levels = np.array([20, -20, 10, -10, 0])
    a = np.random.permutation(np.resize(levels, k // 512 * 4)).reshape(k // 512, 4)
    idx = np.arange(k)
    return np.exp2(a[idx // 512, idx % 128 // 32])


BF16 = ml_dtypes.bfloat16


def bf(x):
    return np.asarray(x, np.float32).astype(BF16)


def f64(x):
    return np.asarray(x).astype(np.float64)


B, C_IN, C_OUT, K_SIZE, STRIDE, PAD, H = 4, 128, 512, 2, 1, 1, 63
H_OUT = (H + 2 * PAD - K_SIZE) // STRIDE + 1
KK = C_IN * K_SIZE * K_SIZE
T = B * H_OUT * H_OUT


def setup_inputs():
    u = mx_kscale(C_OUT)
    x = np.random.standard_normal((B, C_IN, H, H))
    Kf = np.random.uniform(-1.0, 1.0, (KK, C_OUT)) * np.sqrt(3.0 / KK) / u[None, :]
    g = np.random.standard_normal((B, C_OUT, H_OUT, H_OUT)) * np.exp2(np.random.randint(-12, 1, (B, 1, H_OUT, H_OUT))) * 4.0 * u[None, :, None, None]
    return {"x": bf(x), "K": bf(Kf.reshape(K_SIZE, K_SIZE, C_IN, C_OUT)), "grad_out": bf(g)}


def reference(x, K, grad_out):
    gt = f64(grad_out).transpose(0, 2, 3, 1).reshape(T, C_OUT)
    Kf = f64(K).reshape(KK, C_OUT)
    dp = mxq(gt, 1, "e5m2") @ mxq(Kf, 1, "e4m3").T
    dp = dp.reshape(B, H_OUT, H_OUT, C_IN, K_SIZE, K_SIZE)
    end = (H_OUT - 1) * STRIDE + 1
    dxp = np.zeros((B, C_IN, H + 2 * PAD, H + 2 * PAD))
    for di in range(K_SIZE):
        for dj in range(K_SIZE):
            dxp[:, :, di:di + end:STRIDE, dj:dj + end:STRIDE] += dp[:, :, :, :, di, dj].transpose(0, 3, 1, 2)
    return dxp[:, :, PAD:PAD + H, PAD:PAD + H]

@@ -1,0 +1,173 @@
+from contextlib import ExitStack
+
+import concourse.mybir as mybir
+from concourse.masks import make_identity
+
+F32 = mybir.dt.float32
+BF16 = mybir.dt.bfloat16
+U32 = mybir.dt.uint32
+U8 = mybir.dt.uint8
+E4M3_X4 = mybir.dt.float8_e4m3fn_x4
+E5M2_X4 = mybir.dt.float8_e5m2_x4
+
+P = 128
+PACK = 4
+BATCH = 4
+C_OUT = P * PACK
+TAPS = 4
+G_SIDE = 64
+X_SIDE = 63
+PIXELS = G_SIDE * G_SIDE
+N_TILE = 512
+TILE_ROWS = N_TILE // G_SIDE
+CHUNK = 1024
+CHUNK_ROWS = CHUNK // G_SIDE
+CHUNKS = PIXELS // CHUNK
+TILES_IN_CHUNK = CHUNK // N_TILE
+VECTOR_PIXELS = CHUNK // 2
+RUN = 4
+
+FLOPS = 2 * BATCH * PIXELS * C_OUT * TAPS * P
+BYTES = 2 * BATCH * C_OUT * PIXELS + 2 * TAPS * P * C_OUT + 4 * BATCH * P * X_SIDE * X_SIDE
+
+
+def tile_conv2d_t_kernel(tc, x, K, grad_out, out):
+    nc = tc.nc
+    with ExitStack() as ctx:
+        ctx.enter_context(tc.manual_schedule())
+        consts = ctx.enter_context(tc.tile_pool(name="consts", bufs=1))
+        raw_pool = ctx.enter_context(tc.tile_pool(name="raw", bufs=BATCH))
+        grouped_pool = ctx.enter_context(tc.tile_pool(name="grouped", bufs=3))
+        codes_pool = ctx.enter_context(tc.tile_pool(name="codes", bufs=2))
+        shifted_pool = ctx.enter_context(tc.tile_pool(name="shifted", bufs=4))
+        result_pool = ctx.enter_context(tc.tile_pool(name="result", bufs=3))
+        psum = ctx.enter_context(tc.psum_pool(name="psum", bufs=2 * TILES_IN_CHUNK))
+
+        k_raw = consts.tile([P, TAPS * C_OUT], BF16)
+        k_rows = K.rearrange("kh kw c o -> (kh kw c) o")
+        nc.scalar.dma_start(out=k_raw[:], in_=k_rows.rearrange("(c s) o -> c (s o)", s=TAPS))
+        raw = []
+        for b in range(BATCH):
+            raw_b = raw_pool.tile([P, PACK, PIXELS], BF16, name="raw_b")
+            image = grad_out[b].rearrange("(p t) i j -> p t (i j)", t=PACK)
+            pieces = CHUNKS if b == 0 else 1
+            width = PIXELS // pieces
+            for piece in range(pieces):
+                cols = slice(piece * width, (piece + 1) * width)
+                nc.sync.dma_start(out=raw_b[:, :, cols], in_=image[:, :, cols])
+            raw.append(raw_b)
+
+        ident = consts.tile([P, P], F32)
+        make_identity(nc, ident[:])
+        k_words = k_raw[:].bitcast(F32).rearrange("c (s p u) -> c s u p", s=TAPS, u=2)
+        k_grouped = consts.tile([P, TAPS * P * PACK], BF16, align_bytes=64)
+        k_grouped_words = k_grouped[:].bitcast(F32).rearrange("p (s c u) -> p s c u", s=TAPS, u=2)
+        for di in range(2):
+            k_t = psum.tile([P, 2, 2, P], F32, tag="dj%d" % di, name="k_t")
+            for dj in range(2):
+                for u in range(2):
+                    nc.tensor.transpose(k_t[:, dj, u, :], k_words[:, 2 * di + dj, u, :], ident[:])
+            copy_out = nc.vector.tensor_copy if di == 0 else nc.scalar.copy
+            copy_out(
+                out=k_grouped_words[:, 2 * di : 2 * di + 2],
+                in_=k_t[:].rearrange("p s u c -> p s c u"),
+            )
+        k_codes = consts.tile([P, TAPS * P], U32, align_bytes=64)
+        k_scales = consts.tile([P, TAPS * P], U8, align_bytes=64)
+        nc.vector.quantize_mx(out=k_codes[:].bitcast(E4M3_X4), scales=k_scales[:], in_=k_grouped[:])
+
+        grouped = {}
+        g_codes = {}
+        g_scales = {}
+        banks = {}
+
+        def regroup(n):
+            b, h = divmod(n, CHUNKS)
+            grouped[n] = grouped_pool.tile([P, CHUNK * PACK], BF16, align_bytes=64, name="grouped_n")
+            shares = (
+                (nc.vector.tensor_copy, 0, VECTOR_PIXELS),
+                (nc.scalar.copy, VECTOR_PIXELS, CHUNK),
+            )
+            for copy, lo, hi in shares:
+                copy(
+                    out=grouped[n][:, lo * PACK : hi * PACK].rearrange("p (w i t) -> p w t i", i=RUN, t=PACK),
+                    in_=raw[b][:, :, h * CHUNK + lo : h * CHUNK + hi].rearrange("p t (w i) -> p w t i", i=RUN),
+                )
+
+        def quantise(n):
+            b, h = divmod(n, CHUNKS)
+            if h == 0:
+                g_codes[b] = codes_pool.tile([P, PIXELS], U32, align_bytes=64, name="g_codes_b")
+                g_scales[b] = codes_pool.tile([P, PIXELS], U8, align_bytes=64, name="g_scales_b")
+            cols = slice(h * CHUNK, (h + 1) * CHUNK)
+            nc.vector.quantize_mx(
+                out=g_codes[b][:, cols].bitcast(E5M2_X4),
+                scales=g_scales[b][:, cols],
+                in_=grouped[n][:],
+            )
+
+        def first_row(b_tile):
+            return max(TILE_ROWS * b_tile - 1, 0)
+
+        def multiply(n):
+            b, h = divmod(n, CHUNKS)
+            for k in range(TILES_IN_CHUNK):
+                r0 = first_row(TILES_IN_CHUNK * h + k)
+                pair = []
+                for dj in range(2):
+                    acc = psum.tile([P, N_TILE], F32, tag="dj%d" % dj, name="acc")
+                    for di in range(2):
+                        s = 2 * di + dj
+                        tap = slice(s * P, (s + 1) * P)
+                        window = slice((r0 + 1 - di) * G_SIDE, (r0 + 1 - di) * G_SIDE + N_TILE)
+                        nc.tensor.matmul_mx(
+                            out=acc[:],
+                            lhsT=k_codes[:, tap].bitcast(E4M3_X4),
+                            lhsT_scale=k_scales[:, tap],
+                            rhs=g_codes[b][:, window].bitcast(E5M2_X4),
+                            rhs_scale=g_scales[b][:, window],
+                            start=(di == 0),
+                            stop=(di == 1),
+                        )
+                    pair.append(acc[:].rearrange("p (y j) -> p y j", j=G_SIDE))
+                banks[(n, k)] = pair
+
+        shifted = {}
+
+        def copy_shifted(n):
+            h = n % CHUNKS
+            for k in range(TILES_IN_CHUNK):
+                m = TILES_IN_CHUNK * h + k
+                rows = TILE_ROWS * m + TILE_ROWS - 1 - first_row(m)
+                shifted[(n, k)] = shifted_pool.tile([P, TILE_ROWS, X_SIDE], F32, name="shifted_nk")
+                nc.scalar.copy(out=shifted[(n, k)][:, 0:rows, :], in_=banks[(n, k)][0][:, 0:rows, 1:G_SIDE])
+
+        def add_and_store(n):
+            b, h = divmod(n, CHUNKS)
+            chunk_row = first_row(TILES_IN_CHUNK * h)
+            result = result_pool.tile([P, CHUNK_ROWS, X_SIDE], F32, name="result")
+            done = 0
+            for k in range(TILES_IN_CHUNK):
+                m = TILES_IN_CHUNK * h + k
+                rows = TILE_ROWS * m + TILE_ROWS - 1 - first_row(m)
+                nc.vector.tensor_tensor(
+                    out=result[:, done : done + rows, :],
+                    in0=banks[(n, k)][1][:, 0:rows, 0:X_SIDE],
+                    in1=shifted[(n, k)][:, 0:rows, :],
+                    op=mybir.AluOpType.add,
+                )
+                done += rows
+            nc.gpsimd.dma_start(out=out[b, :, chunk_row : chunk_row + done, :], in_=result[:, 0:done, :])
+
+        total = BATCH * CHUNKS
+        regroup(0)
+        for n in range(total + 1):
+            if n >= 1:
+                copy_shifted(n - 1)
+            if n + 1 < total:
+                regroup(n + 1)
+            if n < total:
+                quantise(n)
+                multiply(n)
+            if n >= 1:
+                add_and_store(n - 1)

@@ -24,6 +24,10 @@ CHUNK = 1024
 CHUNK_ROWS = CHUNK // G_SIDE
 CHUNKS = PIXELS // CHUNK
 TILES_IN_CHUNK = CHUNK // N_TILE
+LOAD = 2048
+LOADS = BATCH * PIXELS // LOAD
+CHUNKS_IN_LOAD = LOAD // CHUNK
+RAW_BUFS = 3
 VECTOR_PIXELS = CHUNK // 2
 RUN = 4
 
@@ -36,26 +40,32 @@ def tile_conv2d_t_kernel(tc, x, K, grad_out, out):
     with ExitStack() as ctx:
         ctx.enter_context(tc.manual_schedule())
         consts = ctx.enter_context(tc.tile_pool(name="consts", bufs=1))
-        raw_pool = ctx.enter_context(tc.tile_pool(name="raw", bufs=BATCH))
+        raw_pool = ctx.enter_context(tc.tile_pool(name="raw", bufs=RAW_BUFS))
         grouped_pool = ctx.enter_context(tc.tile_pool(name="grouped", bufs=3))
         codes_pool = ctx.enter_context(tc.tile_pool(name="codes", bufs=2))
         shifted_pool = ctx.enter_context(tc.tile_pool(name="shifted", bufs=4))
-        result_pool = ctx.enter_context(tc.tile_pool(name="result", bufs=3))
+        result_pool = ctx.enter_context(tc.tile_pool(name="result", bufs=4))
         psum = ctx.enter_context(tc.psum_pool(name="psum", bufs=2 * TILES_IN_CHUNK))
 
         k_raw = consts.tile([P, TAPS * C_OUT], BF16)
         k_rows = K.rearrange("kh kw c o -> (kh kw c) o")
-        nc.scalar.dma_start(out=k_raw[:], in_=k_rows.rearrange("(c s) o -> c (s o)", s=TAPS))
-        raw = []
-        for b in range(BATCH):
-            raw_b = raw_pool.tile([P, PACK, PIXELS], BF16, name="raw_b")
+        nc.sync.dma_start(out=k_raw[:], in_=k_rows.rearrange("(c s) o -> c (s o)", s=TAPS))
+        raw = {}
+
+        def load(g):
+            b, half = divmod(g, PIXELS // LOAD)
+            raw[g] = raw_pool.tile([P, PACK, LOAD], BF16, name="raw_g")
             image = grad_out[b].rearrange("(p t) i j -> p t (i j)", t=PACK)
-            pieces = CHUNKS if b == 0 else 1
-            width = PIXELS // pieces
+            pieces = CHUNKS_IN_LOAD if g == 0 else 1
+            width = LOAD // pieces
             for piece in range(pieces):
-                cols = slice(piece * width, (piece + 1) * width)
-                nc.sync.dma_start(out=raw_b[:, :, cols], in_=image[:, :, cols])
-            raw.append(raw_b)
+                nc.sync.dma_start(
+                    out=raw[g][:, :, piece * width : (piece + 1) * width],
+                    in_=image[:, :, half * LOAD + piece * width : half * LOAD + (piece + 1) * width],
+                )
+
+        for g in range(RAW_BUFS):
+            load(g)
 
         ident = consts.tile([P, P], F32)
         make_identity(nc, ident[:])
@@ -82,7 +92,7 @@ def tile_conv2d_t_kernel(tc, x, K, grad_out, out):
         banks = {}
 
         def regroup(n):
-            b, h = divmod(n, CHUNKS)
+            g, part = divmod(n, CHUNKS_IN_LOAD)
             grouped[n] = grouped_pool.tile([P, CHUNK * PACK], BF16, align_bytes=64, name="grouped_n")
             shares = (
                 (nc.vector.tensor_copy, 0, VECTOR_PIXELS),
@@ -91,7 +101,7 @@ def tile_conv2d_t_kernel(tc, x, K, grad_out, out):
             for copy, lo, hi in shares:
                 copy(
                     out=grouped[n][:, lo * PACK : hi * PACK].rearrange("p (w i t) -> p w t i", i=RUN, t=PACK),
-                    in_=raw[b][:, :, h * CHUNK + lo : h * CHUNK + hi].rearrange("p t (w i) -> p w t i", i=RUN),
+                    in_=raw[g][:, :, part * CHUNK + lo : part * CHUNK + hi].rearrange("p t (w i) -> p w t i", i=RUN),
                 )
 
         def quantise(n):
@@ -157,7 +167,7 @@ def tile_conv2d_t_kernel(tc, x, K, grad_out, out):
                     op=mybir.AluOpType.add,
                 )
                 done += rows
-            nc.gpsimd.dma_start(out=out[b, :, chunk_row : chunk_row + done, :], in_=result[:, 0:done, :])
+            nc.sync.dma_start(out=out[b, :, chunk_row : chunk_row + done, :], in_=result[:, 0:done, :])
 
         total = BATCH * CHUNKS
         regroup(0)
@@ -166,6 +176,9 @@ def tile_conv2d_t_kernel(tc, x, K, grad_out, out):
                 copy_shifted(n - 1)
             if n + 1 < total:
                 regroup(n + 1)
+                next_load = (n + 1) // CHUNKS_IN_LOAD + RAW_BUFS
+                if (n + 1) % CHUNKS_IN_LOAD == CHUNKS_IN_LOAD - 1 and next_load < LOADS:
+                    load(next_load)
             if n < total:
                 quantise(n)
                 multiply(n)

@@ -28,7 +28,9 @@ LOAD = 2048
 LOADS = BATCH * PIXELS // LOAD
 CHUNKS_IN_LOAD = LOAD // CHUNK
 RAW_BUFS = 3
-VECTOR_PIXELS = CHUNK // 2
+VECTOR_PIXELS = 352
+SCALAR_PIXELS = 480
+GPSIMD_PIXELS = CHUNK - VECTOR_PIXELS - SCALAR_PIXELS
 RUN = 4
 
 FLOPS = 2 * BATCH * PIXELS * C_OUT * TAPS * P
@@ -94,15 +96,21 @@ def tile_conv2d_t_kernel(tc, x, K, grad_out, out):
         def regroup(n):
             g, part = divmod(n, CHUNKS_IN_LOAD)
             grouped[n] = grouped_pool.tile([P, CHUNK * PACK], BF16, align_bytes=64, name="grouped_n")
-            shares = (
-                (nc.vector.tensor_copy, 0, VECTOR_PIXELS),
-                (nc.scalar.copy, VECTOR_PIXELS, CHUNK),
-            )
-            for copy, lo, hi in shares:
-                copy(
-                    out=grouped[n][:, lo * PACK : hi * PACK].rearrange("p (w i t) -> p w t i", i=RUN, t=PACK),
-                    in_=raw[g][:, :, part * CHUNK + lo : part * CHUNK + hi].rearrange("p t (w i) -> p w t i", i=RUN),
+
+            def share(lo, width):
+                return (
+                    grouped[n][:, lo * PACK : (lo + width) * PACK].rearrange("p (w i t) -> p w t i", i=RUN, t=PACK),
+                    raw[g][:, :, part * CHUNK + lo : part * CHUNK + lo + width].rearrange("p t (w i) -> p w t i", i=RUN),
                 )
+
+            to, source = share(0, VECTOR_PIXELS)
+            nc.vector.tensor_copy(out=to, in_=source)
+            to, source = share(VECTOR_PIXELS, SCALAR_PIXELS)
+            nc.scalar.copy(out=to, in_=source)
+            to, source = share(VECTOR_PIXELS + SCALAR_PIXELS, GPSIMD_PIXELS)
+            nc.gpsimd.tensor_scalar(
+                out=to, in0=source, scalar1=1.0, scalar2=0.0, op0=mybir.AluOpType.mult, op1=mybir.AluOpType.add
+            )
 
         def quantise(n):
             b, h = divmod(n, CHUNKS)

@@ -28,9 +28,7 @@ LOAD = 2048
 LOADS = BATCH * PIXELS // LOAD
 CHUNKS_IN_LOAD = LOAD // CHUNK
 RAW_BUFS = 3
-VECTOR_PIXELS = 352
-SCALAR_PIXELS = 480
-GPSIMD_PIXELS = CHUNK - VECTOR_PIXELS - SCALAR_PIXELS
+VECTOR_PIXELS = CHUNK // 2
 RUN = 4
 
 FLOPS = 2 * BATCH * PIXELS * C_OUT * TAPS * P
@@ -58,7 +56,7 @@ def tile_conv2d_t_kernel(tc, x, K, grad_out, out):
             b, half = divmod(g, PIXELS // LOAD)
             raw[g] = raw_pool.tile([P, PACK, LOAD], BF16, name="raw_g")
             image = grad_out[b].rearrange("(p t) i j -> p t (i j)", t=PACK)
-            pieces = CHUNKS_IN_LOAD if g == 0 else 1
+            pieces = CHUNKS_IN_LOAD if g < RAW_BUFS else 1
             width = LOAD // pieces
             for piece in range(pieces):
                 nc.sync.dma_start(
@@ -96,33 +94,28 @@ def tile_conv2d_t_kernel(tc, x, K, grad_out, out):
         def regroup(n):
             g, part = divmod(n, CHUNKS_IN_LOAD)
             grouped[n] = grouped_pool.tile([P, CHUNK * PACK], BF16, align_bytes=64, name="grouped_n")
-
-            def share(lo, width):
-                return (
-                    grouped[n][:, lo * PACK : (lo + width) * PACK].rearrange("p (w i t) -> p w t i", i=RUN, t=PACK),
-                    raw[g][:, :, part * CHUNK + lo : part * CHUNK + lo + width].rearrange("p t (w i) -> p w t i", i=RUN),
-                )
-
-            to, source = share(0, VECTOR_PIXELS)
-            nc.vector.tensor_copy(out=to, in_=source)
-            to, source = share(VECTOR_PIXELS, SCALAR_PIXELS)
-            nc.scalar.copy(out=to, in_=source)
-            to, source = share(VECTOR_PIXELS + SCALAR_PIXELS, GPSIMD_PIXELS)
-            nc.gpsimd.tensor_scalar(
-                out=to, in0=source, scalar1=1.0, scalar2=0.0, op0=mybir.AluOpType.mult, op1=mybir.AluOpType.add
+            shares = (
+                (nc.vector.tensor_copy, 0, VECTOR_PIXELS),
+                (nc.scalar.copy, VECTOR_PIXELS, CHUNK),
             )
+            for copy, lo, hi in shares:
+                copy(
+                    out=grouped[n][:, lo * PACK : hi * PACK].rearrange("p (w i t) -> p w t i", i=RUN, t=PACK),
+                    in_=raw[g][:, :, part * CHUNK + lo : part * CHUNK + hi].rearrange("p t (w i) -> p w t i", i=RUN),
+                )
 
         def quantise(n):
             b, h = divmod(n, CHUNKS)
             if h == 0:
                 g_codes[b] = codes_pool.tile([P, PIXELS], U32, align_bytes=64, name="g_codes_b")
                 g_scales[b] = codes_pool.tile([P, PIXELS], U8, align_bytes=64, name="g_scales_b")
-            cols = slice(h * CHUNK, (h + 1) * CHUNK)
-            nc.vector.quantize_mx(
-                out=g_codes[b][:, cols].bitcast(E5M2_X4),
-                scales=g_scales[b][:, cols],
-                in_=grouped[n][:],
-            )
+            for k in range(TILES_IN_CHUNK):
+                cols = slice(h * CHUNK + k * N_TILE, h * CHUNK + (k + 1) * N_TILE)
+                nc.vector.quantize_mx(
+                    out=g_codes[b][:, cols].bitcast(E5M2_X4),
+                    scales=g_scales[b][:, cols],
+                    in_=grouped[n][:, k * N_TILE * PACK : (k + 1) * N_TILE * PACK],
+                )
 
         def first_row(b_tile):
             return max(TILE_ROWS * b_tile - 1, 0)
@@ -165,6 +158,7 @@ def tile_conv2d_t_kernel(tc, x, K, grad_out, out):
             chunk_row = first_row(TILES_IN_CHUNK * h)
             result = result_pool.tile([P, CHUNK_ROWS, X_SIDE], F32, name="result")
             done = 0
+            stored = 0
             for k in range(TILES_IN_CHUNK):
                 m = TILES_IN_CHUNK * h + k
                 rows = TILE_ROWS * m + TILE_ROWS - 1 - first_row(m)
@@ -175,7 +169,11 @@ def tile_conv2d_t_kernel(tc, x, K, grad_out, out):
                     op=mybir.AluOpType.add,
                 )
                 done += rows
-            nc.sync.dma_start(out=out[b, :, chunk_row : chunk_row + done, :], in_=result[:, 0:done, :])
+                if k == TILES_IN_CHUNK - 1 or n == total - 1:
+                    nc.sync.dma_start(
+                        out=out[b, :, chunk_row + stored : chunk_row + done, :], in_=result[:, stored:done, :]
+                    )
+                    stored = done
 
         total = BATCH * CHUNKS
         regroup(0)

@@ -28,7 +28,8 @@ LOAD = 2048
 LOADS = BATCH * PIXELS // LOAD
 CHUNKS_IN_LOAD = LOAD // CHUNK
 RAW_BUFS = 3
-VECTOR_PIXELS = CHUNK // 2
+VECTOR_PIXELS = 400
+GPSIMD_PIXELS = 144
 RUN = 4
 
 FLOPS = 2 * BATCH * PIXELS * C_OUT * TAPS * P
@@ -41,7 +42,7 @@ def tile_conv2d_t_kernel(tc, x, K, grad_out, out):
         ctx.enter_context(tc.manual_schedule())
         consts = ctx.enter_context(tc.tile_pool(name="consts", bufs=1))
         raw_pool = ctx.enter_context(tc.tile_pool(name="raw", bufs=RAW_BUFS))
-        grouped_pool = ctx.enter_context(tc.tile_pool(name="grouped", bufs=3))
+        grouped_pool = ctx.enter_context(tc.tile_pool(name="grouped", bufs=2))
         codes_pool = ctx.enter_context(tc.tile_pool(name="codes", bufs=2))
         shifted_pool = ctx.enter_context(tc.tile_pool(name="shifted", bufs=4))
         result_pool = ctx.enter_context(tc.tile_pool(name="result", bufs=4))
@@ -93,16 +94,32 @@ def tile_conv2d_t_kernel(tc, x, K, grad_out, out):
 
         def regroup(n):
             g, part = divmod(n, CHUNKS_IN_LOAD)
-            grouped[n] = grouped_pool.tile([P, CHUNK * PACK], BF16, align_bytes=64, name="grouped_n")
+            vector_end = VECTOR_PIXELS
+            if n not in grouped:
+                grouped[n] = grouped_pool.tile([P, CHUNK * PACK], BF16, align_bytes=64, name="grouped_n")
+                vector_end = VECTOR_PIXELS + GPSIMD_PIXELS
             shares = (
-                (nc.vector.tensor_copy, 0, VECTOR_PIXELS),
-                (nc.scalar.copy, VECTOR_PIXELS, CHUNK),
+                (nc.vector.tensor_copy, 0, vector_end),
+                (nc.scalar.copy, VECTOR_PIXELS + GPSIMD_PIXELS, CHUNK),
             )
             for copy, lo, hi in shares:
                 copy(
                     out=grouped[n][:, lo * PACK : hi * PACK].rearrange("p (w i t) -> p w t i", i=RUN, t=PACK),
                     in_=raw[g][:, :, part * CHUNK + lo : part * CHUNK + hi].rearrange("p t (w i) -> p w t i", i=RUN),
                 )
+
+        def regroup_on_gpsimd(n):
+            g, part = divmod(n, CHUNKS_IN_LOAD)
+            grouped[n] = grouped_pool.tile([P, CHUNK * PACK], BF16, align_bytes=64, name="grouped_n")
+            lo, hi = VECTOR_PIXELS, VECTOR_PIXELS + GPSIMD_PIXELS
+            nc.gpsimd.tensor_scalar(
+                out=grouped[n][:, lo * PACK : hi * PACK].rearrange("p (w t) -> p w t", t=PACK),
+                in0=raw[g][:, :, part * CHUNK + lo : part * CHUNK + hi].rearrange("p t w -> p w t"),
+                scalar1=1.0,
+                scalar2=0.0,
+                op0=mybir.AluOpType.mult,
+                op1=mybir.AluOpType.add,
+            )
 
         def quantise(n):
             b, h = divmod(n, CHUNKS)
@@ -188,5 +205,7 @@ def tile_conv2d_t_kernel(tc, x, K, grad_out, out):
             if n < total:
                 quantise(n)
                 multiply(n)
+            if n + 2 < total:
+                regroup_on_gpsimd(n + 2)
             if n >= 1:
                 add_and_store(n - 1)

@@ -24,12 +24,11 @@ CHUNK = 1024
 CHUNK_ROWS = CHUNK // G_SIDE
 CHUNKS = PIXELS // CHUNK
 TILES_IN_CHUNK = CHUNK // N_TILE
-LOAD = 2048
-LOADS = BATCH * PIXELS // LOAD
-CHUNKS_IN_LOAD = LOAD // CHUNK
-RAW_BUFS = 3
-VECTOR_PIXELS = 400
+RAW_BUFS = 6
+VECTOR_PIXELS = 384
 GPSIMD_PIXELS = 144
+FILL_CHUNKS = 2
+FILL_VECTOR_SHARE = (2, 3)
 RUN = 4
 
 FLOPS = 2 * BATCH * PIXELS * C_OUT * TAPS * P
@@ -50,42 +49,43 @@ def tile_conv2d_t_kernel(tc, x, K, grad_out, out):
 
         k_raw = consts.tile([P, TAPS * C_OUT], BF16)
         k_rows = K.rearrange("kh kw c o -> (kh kw c) o")
-        nc.sync.dma_start(out=k_raw[:], in_=k_rows.rearrange("(c s) o -> c (s o)", s=TAPS))
         raw = {}
 
-        def load(g):
-            b, half = divmod(g, PIXELS // LOAD)
-            raw[g] = raw_pool.tile([P, PACK, LOAD], BF16, name="raw_g")
+        def load(n):
+            b, h = divmod(n, CHUNKS)
+            pieces = TILES_IN_CHUNK if n == 0 else 1
+            width = CHUNK // pieces
+            raw[n] = raw_pool.tile([P, pieces, PACK, width], BF16, name="raw_n")
             image = grad_out[b].rearrange("(p t) i j -> p t (i j)", t=PACK)
-            pieces = CHUNKS_IN_LOAD if g < RAW_BUFS else 1
-            width = LOAD // pieces
             for piece in range(pieces):
-                nc.sync.dma_start(
-                    out=raw[g][:, :, piece * width : (piece + 1) * width],
-                    in_=image[:, :, half * LOAD + piece * width : half * LOAD + (piece + 1) * width],
-                )
+                lo = h * CHUNK + piece * width
+                nc.sync.dma_start(out=raw[n][:, piece], in_=image[:, :, lo : lo + width])
 
-        for g in range(RAW_BUFS):
-            load(g)
+        load(0)
+        nc.sync.dma_start(out=k_raw[:], in_=k_rows.rearrange("(c s) o -> c (s o)", s=TAPS))
+        for n in range(1, RAW_BUFS):
+            load(n)
 
         ident = consts.tile([P, P], F32)
         make_identity(nc, ident[:])
         k_words = k_raw[:].bitcast(F32).rearrange("c (s p u) -> c s u p", s=TAPS, u=2)
         k_grouped = consts.tile([P, TAPS * P * PACK], BF16, align_bytes=64)
         k_grouped_words = k_grouped[:].bitcast(F32).rearrange("p (s c u) -> p s c u", s=TAPS, u=2)
-        for di in range(2):
-            k_t = psum.tile([P, 2, 2, P], F32, tag="dj%d" % di, name="k_t")
-            for dj in range(2):
-                for u in range(2):
-                    nc.tensor.transpose(k_t[:, dj, u, :], k_words[:, 2 * di + dj, u, :], ident[:])
-            copy_out = nc.vector.tensor_copy if di == 0 else nc.scalar.copy
-            copy_out(
-                out=k_grouped_words[:, 2 * di : 2 * di + 2],
-                in_=k_t[:].rearrange("p s u c -> p s c u"),
-            )
         k_codes = consts.tile([P, TAPS * P], U32, align_bytes=64)
         k_scales = consts.tile([P, TAPS * P], U8, align_bytes=64)
-        nc.vector.quantize_mx(out=k_codes[:].bitcast(E4M3_X4), scales=k_scales[:], in_=k_grouped[:])
+
+        def prepare_kernel():
+            for di in range(2):
+                k_t = psum.tile([P, 2, 2, P], F32, tag="dj%d" % di, name="k_t")
+                for dj in range(2):
+                    for u in range(2):
+                        nc.tensor.transpose(k_t[:, dj, u, :], k_words[:, 2 * di + dj, u, :], ident[:])
+                copy_out = nc.vector.tensor_copy if di == 0 else nc.scalar.copy
+                copy_out(
+                    out=k_grouped_words[:, 2 * di : 2 * di + 2],
+                    in_=k_t[:].rearrange("p s u c -> p s c u"),
+                )
+            nc.vector.quantize_mx(out=k_codes[:].bitcast(E4M3_X4), scales=k_scales[:], in_=k_grouped[:])
 
         grouped = {}
         g_codes = {}
@@ -93,28 +93,35 @@ def tile_conv2d_t_kernel(tc, x, K, grad_out, out):
         banks = {}
 
         def regroup(n):
-            g, part = divmod(n, CHUNKS_IN_LOAD)
-            vector_end = VECTOR_PIXELS
-            if n not in grouped:
+            if n >= FILL_CHUNKS:
+                shares = (
+                    (nc.vector.tensor_copy, 0, VECTOR_PIXELS),
+                    (nc.scalar.copy, VECTOR_PIXELS + GPSIMD_PIXELS, CHUNK),
+                )
+            else:
                 grouped[n] = grouped_pool.tile([P, CHUNK * PACK], BF16, align_bytes=64, name="grouped_n")
-                vector_end = VECTOR_PIXELS + GPSIMD_PIXELS
-            shares = (
-                (nc.vector.tensor_copy, 0, vector_end),
-                (nc.scalar.copy, VECTOR_PIXELS + GPSIMD_PIXELS, CHUNK),
-            )
+                width = N_TILE if n == 0 else CHUNK
+                vector_width = width * FILL_VECTOR_SHARE[0] // FILL_VECTOR_SHARE[1] // (2 * RUN) * (2 * RUN)
+                shares = []
+                for lo in range(0, CHUNK, width):
+                    shares.append((nc.vector.tensor_copy, lo, lo + vector_width))
+                    shares.append((nc.scalar.copy, lo + vector_width, lo + width))
+            piece_width = raw[n].shape[3]
             for copy, lo, hi in shares:
+                piece = lo // piece_width
                 copy(
                     out=grouped[n][:, lo * PACK : hi * PACK].rearrange("p (w i t) -> p w t i", i=RUN, t=PACK),
-                    in_=raw[g][:, :, part * CHUNK + lo : part * CHUNK + hi].rearrange("p t (w i) -> p w t i", i=RUN),
+                    in_=raw[n][:, piece, :, lo - piece * piece_width : hi - piece * piece_width].rearrange(
+                        "p t (w i) -> p w t i", i=RUN
+                    ),
                 )
 
         def regroup_on_gpsimd(n):
-            g, part = divmod(n, CHUNKS_IN_LOAD)
             grouped[n] = grouped_pool.tile([P, CHUNK * PACK], BF16, align_bytes=64, name="grouped_n")
             lo, hi = VECTOR_PIXELS, VECTOR_PIXELS + GPSIMD_PIXELS
             nc.gpsimd.tensor_scalar(
                 out=grouped[n][:, lo * PACK : hi * PACK].rearrange("p (w t) -> p w t", t=PACK),
-                in0=raw[g][:, :, part * CHUNK + lo : part * CHUNK + hi].rearrange("p t w -> p w t"),
+                in0=raw[n][:, 0, :, lo:hi].rearrange("p t w -> p w t"),
                 scalar1=1.0,
                 scalar2=0.0,
                 op0=mybir.AluOpType.mult,
@@ -194,16 +201,19 @@ def tile_conv2d_t_kernel(tc, x, K, grad_out, out):
 
         total = BATCH * CHUNKS
         regroup(0)
+        load(RAW_BUFS)
+        quantise(0)
+        prepare_kernel()
         for n in range(total + 1):
             if n >= 1:
                 copy_shifted(n - 1)
             if n + 1 < total:
                 regroup(n + 1)
-                next_load = (n + 1) // CHUNKS_IN_LOAD + RAW_BUFS
-                if (n + 1) % CHUNKS_IN_LOAD == CHUNKS_IN_LOAD - 1 and next_load < LOADS:
-                    load(next_load)
+                if n + 1 + RAW_BUFS < total:
+                    load(n + 1 + RAW_BUFS)
             if n < total:
-                quantise(n)
+                if n >= 1:
+                    quantise(n)
                 multiply(n)
             if n + 2 < total:
                 regroup_on_gpsimd(n + 2)

@@ -25,7 +25,7 @@ CHUNK_ROWS = CHUNK // G_SIDE
 CHUNKS = PIXELS // CHUNK
 TILES_IN_CHUNK = CHUNK // N_TILE
 RAW_BUFS = 6
-VECTOR_PIXELS = 384
+VECTOR_PIXELS = 416
 GPSIMD_PIXELS = 144
 FILL_CHUNKS = 2
 FILL_VECTOR_SHARE = (2, 3)
@@ -44,7 +44,7 @@ def tile_conv2d_t_kernel(tc, x, K, grad_out, out):
         grouped_pool = ctx.enter_context(tc.tile_pool(name="grouped", bufs=2))
         codes_pool = ctx.enter_context(tc.tile_pool(name="codes", bufs=2))
         shifted_pool = ctx.enter_context(tc.tile_pool(name="shifted", bufs=4))
-        result_pool = ctx.enter_context(tc.tile_pool(name="result", bufs=4))
+        result_pool = ctx.enter_context(tc.tile_pool(name="result", bufs=8))
         psum = ctx.enter_context(tc.psum_pool(name="psum", bufs=2 * TILES_IN_CHUNK))
 
         k_raw = consts.tile([P, TAPS * C_OUT], BF16)

@@ -29,7 +29,7 @@ VECTOR_PIXELS = 416
 GPSIMD_PIXELS = 144
 FILL_CHUNKS = 2
 FILL_VECTOR_SHARE = (2, 3)
-RUN = 4
+RUN = 8
 
 FLOPS = 2 * BATCH * PIXELS * C_OUT * TAPS * P
 BYTES = 2 * BATCH * C_OUT * PIXELS + 2 * TAPS * P * C_OUT + 4 * BATCH * P * X_SIDE * X_SIDE

@@ -25,8 +25,8 @@ CHUNK_ROWS = CHUNK // G_SIDE
 CHUNKS = PIXELS // CHUNK
 TILES_IN_CHUNK = CHUNK // N_TILE
 RAW_BUFS = 6
-VECTOR_PIXELS = 416
-GPSIMD_PIXELS = 144
+VECTOR_PIXELS = 400
+GPSIMD_PIXELS = 176
 FILL_CHUNKS = 2
 FILL_VECTOR_SHARE = (2, 3)
 RUN = 8

@@ -24,7 +24,7 @@ CHUNK = 1024
 CHUNK_ROWS = CHUNK // G_SIDE
 CHUNKS = PIXELS // CHUNK
 TILES_IN_CHUNK = CHUNK // N_TILE
-RAW_BUFS = 6
+RAW_BUFS = 12
 VECTOR_PIXELS = 400
 GPSIMD_PIXELS = 176
 FILL_CHUNKS = 2
@@ -44,7 +44,7 @@ def tile_conv2d_t_kernel(tc, x, K, grad_out, out):
         grouped_pool = ctx.enter_context(tc.tile_pool(name="grouped", bufs=2))
         codes_pool = ctx.enter_context(tc.tile_pool(name="codes", bufs=2))
         shifted_pool = ctx.enter_context(tc.tile_pool(name="shifted", bufs=4))
-        result_pool = ctx.enter_context(tc.tile_pool(name="result", bufs=8))
+        result_pool = ctx.enter_context(tc.tile_pool(name="result", bufs=14))
         psum = ctx.enter_context(tc.psum_pool(name="psum", bufs=2 * TILES_IN_CHUNK))
 
         k_raw = consts.tile([P, TAPS * C_OUT], BF16)

@@ -44,7 +44,7 @@ def tile_conv2d_t_kernel(tc, x, K, grad_out, out):
         grouped_pool = ctx.enter_context(tc.tile_pool(name="grouped", bufs=2))
         codes_pool = ctx.enter_context(tc.tile_pool(name="codes", bufs=2))
         shifted_pool = ctx.enter_context(tc.tile_pool(name="shifted", bufs=4))
-        result_pool = ctx.enter_context(tc.tile_pool(name="result", bufs=14))
+        result_pool = ctx.enter_context(tc.tile_pool(name="result", bufs=3))
         psum = ctx.enter_context(tc.psum_pool(name="psum", bufs=2 * TILES_IN_CHUNK))
 
         k_raw = consts.tile([P, TAPS * C_OUT], BF16)
@@ -177,27 +177,33 @@ def tile_conv2d_t_kernel(tc, x, K, grad_out, out):
                 shifted[(n, k)] = shifted_pool.tile([P, TILE_ROWS, X_SIDE], F32, name="shifted_nk")
                 nc.scalar.copy(out=shifted[(n, k)][:, 0:rows, :], in_=banks[(n, k)][0][:, 0:rows, 1:G_SIDE])
 
+        result = {}
+        stored_rows = {}
+
         def add_and_store(n):
             b, h = divmod(n, CHUNKS)
-            chunk_row = first_row(TILES_IN_CHUNK * h)
-            result = result_pool.tile([P, CHUNK_ROWS, X_SIDE], F32, name="result")
-            done = 0
-            stored = 0
+            if h == 0:
+                result[b] = result_pool.tile([P, X_SIDE, X_SIDE], F32, name="result_b")
+                stored_rows[b] = 0
             for k in range(TILES_IN_CHUNK):
                 m = TILES_IN_CHUNK * h + k
-                rows = TILE_ROWS * m + TILE_ROWS - 1 - first_row(m)
+                r0 = first_row(m)
+                r1 = TILE_ROWS * m + TILE_ROWS - 1
                 nc.vector.tensor_tensor(
-                    out=result[:, done : done + rows, :],
-                    in0=banks[(n, k)][1][:, 0:rows, 0:X_SIDE],
-                    in1=shifted[(n, k)][:, 0:rows, :],
+                    out=result[b][:, r0:r1, :],
+                    in0=banks[(n, k)][1][:, 0 : r1 - r0, 0:X_SIDE],
+                    in1=shifted[(n, k)][:, 0 : r1 - r0, :],
                     op=mybir.AluOpType.add,
                 )
-                done += rows
-                if k == TILES_IN_CHUNK - 1 or n == total - 1:
+                if b < BATCH - 1:
+                    store_now = r1 == X_SIDE
+                else:
+                    store_now = k == TILES_IN_CHUNK - 1 or n == total - 1
+                if store_now:
                     nc.sync.dma_start(
-                        out=out[b, :, chunk_row + stored : chunk_row + done, :], in_=result[:, stored:done, :]
+                        out=out[b, :, stored_rows[b] : r1, :], in_=result[b][:, stored_rows[b] : r1, :]
                     )
-                    stored = done
+                    stored_rows[b] = r1
 
         total = BATCH * CHUNKS
         regroup(0)

@@ -25,7 +25,7 @@ CHUNK_ROWS = CHUNK // G_SIDE
 CHUNKS = PIXELS // CHUNK
 TILES_IN_CHUNK = CHUNK // N_TILE
 RAW_BUFS = 12
-VECTOR_PIXELS = 400
+VECTOR_PIXELS = 384
 GPSIMD_PIXELS = 176
 FILL_CHUNKS = 2
 FILL_VECTOR_SHARE = (2, 3)

@@ -25,8 +25,8 @@ CHUNK_ROWS = CHUNK // G_SIDE
 CHUNKS = PIXELS // CHUNK
 TILES_IN_CHUNK = CHUNK // N_TILE
 RAW_BUFS = 12
-VECTOR_PIXELS = 384
-GPSIMD_PIXELS = 176
+VECTOR_PIXELS = 368
+GPSIMD_PIXELS = 192
 FILL_CHUNKS = 2
 FILL_VECTOR_SHARE = (2, 3)
 RUN = 8

from contextlib import ExitStack

import concourse.mybir as mybir
from concourse.masks import make_identity

F32 = mybir.dt.float32
BF16 = mybir.dt.bfloat16
U32 = mybir.dt.uint32
U8 = mybir.dt.uint8
E4M3_X4 = mybir.dt.float8_e4m3fn_x4
E5M2_X4 = mybir.dt.float8_e5m2_x4

P = 128
PACK = 4
BATCH = 4
C_OUT = P * PACK
TAPS = 4
G_SIDE = 64
X_SIDE = 63
PIXELS = G_SIDE * G_SIDE
N_TILE = 512
TILE_ROWS = N_TILE // G_SIDE
CHUNK = 1024
CHUNK_ROWS = CHUNK // G_SIDE
CHUNKS = PIXELS // CHUNK
TILES_IN_CHUNK = CHUNK // N_TILE
RAW_BUFS = 12
VECTOR_PIXELS = 368
GPSIMD_PIXELS = 192
FILL_CHUNKS = 2
FILL_VECTOR_SHARE = (2, 3)
RUN = 8

FLOPS = 2 * BATCH * PIXELS * C_OUT * TAPS * P
BYTES = 2 * BATCH * C_OUT * PIXELS + 2 * TAPS * P * C_OUT + 4 * BATCH * P * X_SIDE * X_SIDE


def tile_conv2d_t_kernel(tc, x, K, grad_out, out):
    nc = tc.nc
    with ExitStack() as ctx:
        ctx.enter_context(tc.manual_schedule())
        consts = ctx.enter_context(tc.tile_pool(name="consts", bufs=1))
        raw_pool = ctx.enter_context(tc.tile_pool(name="raw", bufs=RAW_BUFS))
        grouped_pool = ctx.enter_context(tc.tile_pool(name="grouped", bufs=2))
        codes_pool = ctx.enter_context(tc.tile_pool(name="codes", bufs=2))
        shifted_pool = ctx.enter_context(tc.tile_pool(name="shifted", bufs=4))
        result_pool = ctx.enter_context(tc.tile_pool(name="result", bufs=3))
        psum = ctx.enter_context(tc.psum_pool(name="psum", bufs=2 * TILES_IN_CHUNK))

        k_raw = consts.tile([P, TAPS * C_OUT], BF16)
        k_rows = K.rearrange("kh kw c o -> (kh kw c) o")
        raw = {}

        def load(n):
            b, h = divmod(n, CHUNKS)
            pieces = TILES_IN_CHUNK if n == 0 else 1
            width = CHUNK // pieces
            raw[n] = raw_pool.tile([P, pieces, PACK, width], BF16, name="raw_n")
            image = grad_out[b].rearrange("(p t) i j -> p t (i j)", t=PACK)
            for piece in range(pieces):
                lo = h * CHUNK + piece * width
                nc.sync.dma_start(out=raw[n][:, piece], in_=image[:, :, lo : lo + width])

        load(0)
        nc.sync.dma_start(out=k_raw[:], in_=k_rows.rearrange("(c s) o -> c (s o)", s=TAPS))
        for n in range(1, RAW_BUFS):
            load(n)

        ident = consts.tile([P, P], F32)
        make_identity(nc, ident[:])
        k_words = k_raw[:].bitcast(F32).rearrange("c (s p u) -> c s u p", s=TAPS, u=2)
        k_grouped = consts.tile([P, TAPS * P * PACK], BF16, align_bytes=64)
        k_grouped_words = k_grouped[:].bitcast(F32).rearrange("p (s c u) -> p s c u", s=TAPS, u=2)
        k_codes = consts.tile([P, TAPS * P], U32, align_bytes=64)
        k_scales = consts.tile([P, TAPS * P], U8, align_bytes=64)

        def prepare_kernel():
            for di in range(2):
                k_t = psum.tile([P, 2, 2, P], F32, tag="dj%d" % di, name="k_t")
                for dj in range(2):
                    for u in range(2):
                        nc.tensor.transpose(k_t[:, dj, u, :], k_words[:, 2 * di + dj, u, :], ident[:])
                copy_out = nc.vector.tensor_copy if di == 0 else nc.scalar.copy
                copy_out(
                    out=k_grouped_words[:, 2 * di : 2 * di + 2],
                    in_=k_t[:].rearrange("p s u c -> p s c u"),
                )
            nc.vector.quantize_mx(out=k_codes[:].bitcast(E4M3_X4), scales=k_scales[:], in_=k_grouped[:])

        grouped = {}
        g_codes = {}
        g_scales = {}
        banks = {}

        def regroup(n):
            if n >= FILL_CHUNKS:
                shares = (
                    (nc.vector.tensor_copy, 0, VECTOR_PIXELS),
                    (nc.scalar.copy, VECTOR_PIXELS + GPSIMD_PIXELS, CHUNK),
                )
            else:
                grouped[n] = grouped_pool.tile([P, CHUNK * PACK], BF16, align_bytes=64, name="grouped_n")
                width = N_TILE if n == 0 else CHUNK
                vector_width = width * FILL_VECTOR_SHARE[0] // FILL_VECTOR_SHARE[1] // (2 * RUN) * (2 * RUN)
                shares = []
                for lo in range(0, CHUNK, width):
                    shares.append((nc.vector.tensor_copy, lo, lo + vector_width))
                    shares.append((nc.scalar.copy, lo + vector_width, lo + width))
            piece_width = raw[n].shape[3]
            for copy, lo, hi in shares:
                piece = lo // piece_width
                copy(
                    out=grouped[n][:, lo * PACK : hi * PACK].rearrange("p (w i t) -> p w t i", i=RUN, t=PACK),
                    in_=raw[n][:, piece, :, lo - piece * piece_width : hi - piece * piece_width].rearrange(
                        "p t (w i) -> p w t i", i=RUN
                    ),
                )

        def regroup_on_gpsimd(n):
            grouped[n] = grouped_pool.tile([P, CHUNK * PACK], BF16, align_bytes=64, name="grouped_n")
            lo, hi = VECTOR_PIXELS, VECTOR_PIXELS + GPSIMD_PIXELS
            nc.gpsimd.tensor_scalar(
                out=grouped[n][:, lo * PACK : hi * PACK].rearrange("p (w t) -> p w t", t=PACK),
                in0=raw[n][:, 0, :, lo:hi].rearrange("p t w -> p w t"),
                scalar1=1.0,
                scalar2=0.0,
                op0=mybir.AluOpType.mult,
                op1=mybir.AluOpType.add,
            )

        def quantise(n):
            b, h = divmod(n, CHUNKS)
            if h == 0:
                g_codes[b] = codes_pool.tile([P, PIXELS], U32, align_bytes=64, name="g_codes_b")
                g_scales[b] = codes_pool.tile([P, PIXELS], U8, align_bytes=64, name="g_scales_b")
            for k in range(TILES_IN_CHUNK):
                cols = slice(h * CHUNK + k * N_TILE, h * CHUNK + (k + 1) * N_TILE)
                nc.vector.quantize_mx(
                    out=g_codes[b][:, cols].bitcast(E5M2_X4),
                    scales=g_scales[b][:, cols],
                    in_=grouped[n][:, k * N_TILE * PACK : (k + 1) * N_TILE * PACK],
                )

        def first_row(b_tile):
            return max(TILE_ROWS * b_tile - 1, 0)

        def multiply(n):
            b, h = divmod(n, CHUNKS)
            for k in range(TILES_IN_CHUNK):
                r0 = first_row(TILES_IN_CHUNK * h + k)
                pair = []
                for dj in range(2):
                    acc = psum.tile([P, N_TILE], F32, tag="dj%d" % dj, name="acc")
                    for di in range(2):
                        s = 2 * di + dj
                        tap = slice(s * P, (s + 1) * P)
                        window = slice((r0 + 1 - di) * G_SIDE, (r0 + 1 - di) * G_SIDE + N_TILE)
                        nc.tensor.matmul_mx(
                            out=acc[:],
                            lhsT=k_codes[:, tap].bitcast(E4M3_X4),
                            lhsT_scale=k_scales[:, tap],
                            rhs=g_codes[b][:, window].bitcast(E5M2_X4),
                            rhs_scale=g_scales[b][:, window],
                            start=(di == 0),
                            stop=(di == 1),
                        )
                    pair.append(acc[:].rearrange("p (y j) -> p y j", j=G_SIDE))
                banks[(n, k)] = pair

        shifted = {}

        def copy_shifted(n):
            h = n % CHUNKS
            for k in range(TILES_IN_CHUNK):
                m = TILES_IN_CHUNK * h + k
                rows = TILE_ROWS * m + TILE_ROWS - 1 - first_row(m)
                shifted[(n, k)] = shifted_pool.tile([P, TILE_ROWS, X_SIDE], F32, name="shifted_nk")
                nc.scalar.copy(out=shifted[(n, k)][:, 0:rows, :], in_=banks[(n, k)][0][:, 0:rows, 1:G_SIDE])

        result = {}
        stored_rows = {}

        def add_and_store(n):
            b, h = divmod(n, CHUNKS)
            if h == 0:
                result[b] = result_pool.tile([P, X_SIDE, X_SIDE], F32, name="result_b")
                stored_rows[b] = 0
            for k in range(TILES_IN_CHUNK):
                m = TILES_IN_CHUNK * h + k
                r0 = first_row(m)
                r1 = TILE_ROWS * m + TILE_ROWS - 1
                nc.vector.tensor_tensor(
                    out=result[b][:, r0:r1, :],
                    in0=banks[(n, k)][1][:, 0 : r1 - r0, 0:X_SIDE],
                    in1=shifted[(n, k)][:, 0 : r1 - r0, :],
                    op=mybir.AluOpType.add,
                )
                if b < BATCH - 1:
                    store_now = r1 == X_SIDE
                else:
                    store_now = k == TILES_IN_CHUNK - 1 or n == total - 1
                if store_now:
                    nc.sync.dma_start(
                        out=out[b, :, stored_rows[b] : r1, :], in_=result[b][:, stored_rows[b] : r1, :]
                    )
                    stored_rows[b] = r1

        total = BATCH * CHUNKS
        regroup(0)
        load(RAW_BUFS)
        quantise(0)
        prepare_kernel()
        for n in range(total + 1):
            if n >= 1:
                copy_shifted(n - 1)
            if n + 1 < total:
                regroup(n + 1)
                if n + 1 + RAW_BUFS < total:
                    load(n + 1 + RAW_BUFS)
            if n < total:
                if n >= 1:
                    quantise(n)
                multiply(n)
            if n + 2 < total:
                regroup_on_gpsimd(n + 2)
            if n >= 1:
                add_and_store(n - 1)
